import numpy as np
import ml_dtypes


def mxq(x, axis, fmt="e4m3"):
    dtype, down = {"e4m3": (ml_dtypes.float8_e4m3fn, 7), "e5m2": (ml_dtypes.float8_e5m2, 14)}[fmt]
    v = np.moveaxis(np.asarray(x, np.float32).astype(ml_dtypes.bfloat16).astype(np.float64), axis, -1)
    blocks = v.reshape(v.shape[:-1] + (-1, 32))
    amax = np.abs(blocks).max(-1, keepdims=True)
    byte = np.maximum(np.where(amax > 0, np.frexp(amax)[1] - 1 + 127, 0) - down, 1)
    scale = np.exp2(byte - 127.0)
    codes = (blocks / scale).astype(np.float32).astype(dtype).astype(np.float64)
    return np.moveaxis((codes * scale).reshape(v.shape), -1, axis)


WIDE = False


def mx_kscale(k):
    if not WIDE:
        return np.ones(k)
    levels = np.array([20, -20, 10, -10, 0])
    a = np.random.permutation(np.resize(levels, k // 512 * 4)).reshape(k // 512, 4)
    idx = np.arange(k)
    return np.exp2(a[idx // 512, idx % 128 // 32])


BF16 = ml_dtypes.bfloat16


def bf(x):
    return np.asarray(x, np.float32).astype(BF16)


def f64(x):
    return np.asarray(x).astype(np.float64)


B, S, H, O, W = 8, 1024, 512, 2048, 8


def setup_inputs():
    u = mx_kscale(O)
    hidden_states = np.random.standard_normal((B, S, H))
    gate_proj = np.random.standard_normal((O, H)) / np.sqrt(H) / u[:, None]
    n = B * S // W
    g = np.random.standard_normal((n, O)) * np.exp2(np.random.randint(-12, 1, (n, 1))) * 8.0 * u[None, :]
    return {"hidden_states": bf(hidden_states), "gate_proj": bf(gate_proj),
            "world_size": W, "grad_out": bf(g)}


def reference(hidden_states, gate_proj, world_size, grad_out):
    gv = mxq(f64(grad_out), 1, "e5m2") @ mxq(f64(gate_proj), 0, "e4m3")
    n, h = gv.shape
    return np.broadcast_to(gv[None], (world_size, n, h)).reshape(hidden_states.shape).copy()

@@ -1,0 +1,171 @@
+from contextlib import ExitStack
+
+import concourse.mybir as mybir
+from concourse.masks import make_identity
+
+BF16 = mybir.dt.bfloat16
+F32 = mybir.dt.float32
+U32 = mybir.dt.uint32
+U8 = mybir.dt.uint8
+E4M3X4 = mybir.dt.float8_e4m3fn_x4
+E5M2X4 = mybir.dt.float8_e5m2_x4
+
+P = 128
+N_ROWS = 1024
+K = 2048
+H = 512
+CHUNKS = 8
+TILES = N_ROWS // P
+PASSES = K // 512
+
+FLOPS = 2 * N_ROWS * K * H
+BYTES = 2 * (N_ROWS * K + K * H) + 4 * CHUNKS * N_ROWS * H
+
+FIRST = 3
+PIN = True
+VSHARE = 256
+GROUPS = [[0,3],[3,8]]
+AHEAD = 2
+RES_FIRST = "svsvsvsv"
+RES_REST = "vvvvvvvv"
+COPY_REST = "ss"
+
+
+def tile_testmmrsmodel_t_kernel(tc, hidden_states, gate_proj, world_size, grad_out, out):
+    nc = tc.nc
+    with ExitStack() as ctx:
+        keep = ctx.enter_context(tc.tile_pool(name="keep", bufs=1))
+        psum_t = ctx.enter_context(tc.psum_pool(name="psum_t", bufs=4))
+        psum_a = ctx.enter_context(tc.psum_pool(name="psum_a", bufs=4))
+        if PIN:
+            ctx.enter_context(tc.manual_schedule())
+
+        x_rows = grad_out.rearrange("(p t) k -> p t k", t=TILES)
+        x_raw = [keep.tile([P, K], BF16, name="x_raw%d" % t) for t in range(TILES)]
+        g_raw = [keep.tile([P, 4, H], BF16, name="g_raw%d" % g) for g in range(PASSES)]
+
+        def load_x(t):
+            nc.sync.dma_start(out=x_raw[t][:], in_=x_rows[:, t, :])
+
+        def load_g(g):
+            nc.sync.dma_start(
+                out=g_raw[g][:].rearrange("p (u e) c -> p u e c", u=2),
+                in_=gate_proj[512 * g : 512 * (g + 1), :].rearrange("(u q e) c -> q u e c", u=2, e=2),
+            )
+
+        for t in range(FIRST):
+            load_x(t)
+        for g in range(PASSES):
+            load_g(g)
+        for t in range(FIRST, TILES):
+            load_x(t)
+
+        ident = keep.tile([P, P], F32, name="ident")
+        make_identity(nc, ident[:])
+
+        x_grp = [keep.tile([P, K], BF16, name="x_grp%d" % t, align_bytes=64) for t in range(TILES)]
+        x_code = [keep.tile([P, K // 4], U32, name="x_code%d" % t, align_bytes=64) for t in range(TILES)]
+        x_scale = [keep.tile([P, K // 4], U8, name="x_scale%d" % t, align_bytes=64) for t in range(TILES)]
+        g_grp = [keep.tile([P, H, 4], BF16, name="g_grp%d" % g, align_bytes=64) for g in range(PASSES)]
+        g_code = [keep.tile([P, H], U32, name="g_code%d" % g, align_bytes=64) for g in range(PASSES)]
+        g_scale = [keep.tile([P, H], U8, name="g_scale%d" % g, align_bytes=64) for g in range(PASSES)]
+        res = [keep.tile([P, hi - lo, H], F32, name="res%d" % lo) for lo, hi in GROUPS]
+        banks = {}
+        accs = {}
+
+        def transposes(t):
+            words = x_raw[t][:].bitcast(F32)
+            for half in range(2):
+                bank = psum_t.tile([P, 2, 2, P], F32, name="xt", tag="xt")
+                banks[(t, half)] = bank
+                for gg in range(2):
+                    for u in range(2):
+                        col = 256 * (2 * half + gg) + 128 * u
+                        nc.tensor.transpose(bank[:, gg, u, :], words[:, col : col + P], ident[:])
+
+        def copy_out(t, half, engine):
+            dst = x_grp[t][:].bitcast(F32).rearrange("p (g r u) -> p g r u", g=PASSES, u=2)
+            src = banks[(t, half)][:].rearrange("p g u r -> p g r u")
+            if engine == "v":
+                nc.vector.tensor_copy(out=dst[:, 2 * half : 2 * half + 2], in_=src)
+            else:
+                nc.scalar.copy(out=dst[:, 2 * half : 2 * half + 2], in_=src)
+
+        def quant_x(t):
+            nc.vector.quantize_mx(out=x_code[t][:].bitcast(E5M2X4), scales=x_scale[t][:], in_=x_grp[t][:])
+
+        def regroup(g):
+            dst = g_grp[g][:].rearrange("p (c i) t -> p c t i", i=4)
+            src = g_raw[g][:].rearrange("p t (c i) -> p c t i", i=4)
+            cut = VSHARE // 4
+            nc.vector.tensor_copy(out=dst[:, 0:cut], in_=src[:, 0:cut])
+            if cut < H // 4:
+                nc.scalar.copy(out=dst[:, cut:], in_=src[:, cut:])
+
+        def quant_g(g):
+            nc.vector.quantize_mx(
+                out=g_code[g][:].bitcast(E4M3X4),
+                scales=g_scale[g][:],
+                in_=g_grp[g][:].rearrange("p c t -> p (c t)"),
+            )
+
+        def mx_pass(t, g):
+            if g == 0:
+                accs[t] = psum_a.tile([P, H], F32, name="acc", tag="acc")
+            nc.tensor.matmul_mx(
+                out=accs[t][:],
+                lhsT=x_code[t][:, P * g : P * (g + 1)].bitcast(E5M2X4),
+                lhsT_scale=x_scale[t][:, P * g : P * (g + 1)],
+                rhs=g_code[g][:].bitcast(E4M3X4),
+                rhs_scale=g_scale[g][:],
+                start=(g == 0),
+                stop=(g == PASSES - 1),
+            )
+
+        def result(t, engine):
+            for i, (lo, hi) in enumerate(GROUPS):
+                if lo <= t < hi:
+                    if engine == "v":
+                        nc.vector.tensor_copy(out=res[i][:, t - lo, :], in_=accs[t][:])
+                    else:
+                        nc.scalar.copy(out=res[i][:, t - lo, :], in_=accs[t][:])
+                    if t == hi - 1:
+                        for r in range(CHUNKS):
+                            nc.sync.dma_start(
+                                out=out[r].rearrange("(p t) h -> p t h", t=TILES)[:, lo:hi, :], in_=res[i][:]
+                            )
+
+        def flip(t):
+            transposes(t)
+            copy_out(t, 0, COPY_REST[0])
+            copy_out(t, 1, COPY_REST[1])
+
+        for t in range(FIRST):
+            transposes(t)
+            copy_out(t, 0, "s")
+            copy_out(t, 1, "v")
+            if t > 0:
+                quant_x(t - 1)
+        regroup(0)
+        quant_x(FIRST - 1)
+        for g in range(1, PASSES):
+            regroup(g)
+            quant_g(g - 1)
+            for t in range(FIRST):
+                mx_pass(t, g - 1)
+        quant_g(PASSES - 1)
+        for t in range(FIRST):
+            mx_pass(t, PASSES - 1)
+        for t in range(FIRST):
+            result(t, RES_FIRST[t])
+        for t in range(FIRST, min(FIRST + AHEAD, TILES)):
+            flip(t)
+        quant_x(FIRST)
+        for t in range(FIRST, TILES):
+            if t + AHEAD < TILES:
+                flip(t + AHEAD)
+            if t + 1 < TILES:
+                quant_x(t + 1)
+            for g in range(PASSES):
+                mx_pass(t, g)
+            result(t, RES_REST[t])

@@ -21,10 +21,12 @@ PASSES = K // 512
 FLOPS = 2 * N_ROWS * K * H
 BYTES = 2 * (N_ROWS * K + K * H) + 4 * CHUNKS * N_ROWS * H
 
-FIRST = 3
+FIRST = 2
 PIN = True
-VSHARE = 256
-GROUPS = [[0,3],[3,8]]
+VSHARE = [256,256,256,256]
+X_LOADS = [[0,1],[1,1],[2,1],[3,1],[4,1],[5,1],[6,1],[7,1]]
+GATE_AFTER = 2
+EARLY = [0,3,1,1,1,1,0]
 AHEAD = 2
 RES_FIRST = "svsvsvsv"
 RES_REST = "vvvvvvvv"
@@ -41,11 +43,14 @@ def tile_testmmrsmodel_t_kernel(tc, hidden_states, gate_proj, world_size, grad_o
             ctx.enter_context(tc.manual_schedule())
 
         x_rows = grad_out.rearrange("(p t) k -> p t k", t=TILES)
-        x_raw = [keep.tile([P, K], BF16, name="x_raw%d" % t) for t in range(TILES)]
+        x_raw = {}
         g_raw = [keep.tile([P, 4, H], BF16, name="g_raw%d" % g) for g in range(PASSES)]
 
-        def load_x(t):
-            nc.sync.dma_start(out=x_raw[t][:], in_=x_rows[:, t, :])
+        def load_x(lo, n):
+            raw = keep.tile([P, n, K], BF16, name="x_raw%d" % lo)
+            nc.sync.dma_start(out=raw[:], in_=x_rows[:, lo : lo + n, :])
+            for j in range(n):
+                x_raw[lo + j] = raw[:, j, :]
 
         def load_g(g):
             nc.sync.dma_start(
@@ -53,12 +58,12 @@ def tile_testmmrsmodel_t_kernel(tc, hidden_states, gate_proj, world_size, grad_o
                 in_=gate_proj[512 * g : 512 * (g + 1), :].rearrange("(u q e) c -> q u e c", u=2, e=2),
             )
 
-        for t in range(FIRST):
-            load_x(t)
+        for lo, n in X_LOADS[:GATE_AFTER]:
+            load_x(lo, n)
         for g in range(PASSES):
             load_g(g)
-        for t in range(FIRST, TILES):
-            load_x(t)
+        for lo, n in X_LOADS[GATE_AFTER:]:
+            load_x(lo, n)
 
         ident = keep.tile([P, P], F32, name="ident")
         make_identity(nc, ident[:])
@@ -69,12 +74,13 @@ def tile_testmmrsmodel_t_kernel(tc, hidden_states, gate_proj, world_size, grad_o
         g_grp = [keep.tile([P, H, 4], BF16, name="g_grp%d" % g, align_bytes=64) for g in range(PASSES)]
         g_code = [keep.tile([P, H], U32, name="g_code%d" % g, align_bytes=64) for g in range(PASSES)]
         g_scale = [keep.tile([P, H], U8, name="g_scale%d" % g, align_bytes=64) for g in range(PASSES)]
-        res = [keep.tile([P, hi - lo, H], F32, name="res%d" % lo) for lo, hi in GROUPS]
+        res = keep.tile([P, TILES, H], F32, name="res")
         banks = {}
         accs = {}
+        stored = []
 
         def transposes(t):
-            words = x_raw[t][:].bitcast(F32)
+            words = x_raw[t].bitcast(F32)
             for half in range(2):
                 bank = psum_t.tile([P, 2, 2, P], F32, name="xt", tag="xt")
                 banks[(t, half)] = bank
@@ -97,7 +103,7 @@ def tile_testmmrsmodel_t_kernel(tc, hidden_states, gate_proj, world_size, grad_o
         def regroup(g):
             dst = g_grp[g][:].rearrange("p (c i) t -> p c t i", i=4)
             src = g_raw[g][:].rearrange("p t (c i) -> p c t i", i=4)
-            cut = VSHARE // 4
+            cut = VSHARE[g] // 4
             nc.vector.tensor_copy(out=dst[:, 0:cut], in_=src[:, 0:cut])
             if cut < H // 4:
                 nc.scalar.copy(out=dst[:, cut:], in_=src[:, cut:])
@@ -122,18 +128,25 @@ def tile_testmmrsmodel_t_kernel(tc, hidden_states, gate_proj, world_size, grad_o
                 stop=(g == PASSES - 1),
             )
 
+        def store(r, lo, hi):
+            nc.sync.dma_start(
+                out=out[r].rearrange("(p t) h -> p t h", t=TILES)[:, lo:hi, :], in_=res[:, lo:hi, :]
+            )
+
         def result(t, engine):
-            for i, (lo, hi) in enumerate(GROUPS):
-                if lo <= t < hi:
-                    if engine == "v":
-                        nc.vector.tensor_copy(out=res[i][:, t - lo, :], in_=accs[t][:])
-                    else:
-                        nc.scalar.copy(out=res[i][:, t - lo, :], in_=accs[t][:])
-                    if t == hi - 1:
-                        for r in range(CHUNKS):
-                            nc.sync.dma_start(
-                                out=out[r].rearrange("(p t) h -> p t h", t=TILES)[:, lo:hi, :], in_=res[i][:]
-                            )
+            if engine == "v":
+                nc.vector.tensor_copy(out=res[:, t, :], in_=accs[t][:])
+            else:
+                nc.scalar.copy(out=res[:, t, :], in_=accs[t][:])
+            if t < TILES - 1:
+                for i in range(EARLY[t]):
+                    store(len(stored), 0, t + 1)
+                    stored.append(t + 1)
+            else:
+                for r in range(len(stored), CHUNKS):
+                    store(r, 0, TILES)
+                for r in range(len(stored)):
+                    store(r, stored[r], TILES)
 
         def flip(t):
             transposes(t)

@@ -24,12 +24,13 @@ BYTES = 2 * (N_ROWS * K + K * H) + 4 * CHUNKS * N_ROWS * H
 FIRST = 2
 PIN = True
 VSHARE = [256,256,256,256]
-X_LOADS = [[0,1],[1,1],[2,1],[3,1],[4,1],[5,1],[6,1],[7,1]]
-GATE_AFTER = 2
-EARLY = [0,3,1,1,1,1,0]
+X_LOADS = [[0,2],[2,2],[4,2],[6,2]]
+GATE_AFTER = 1
+EARLY = [0,3,1,1,1,1,1]
 AHEAD = 2
 RES_FIRST = "svsvsvsv"
 RES_REST = "vvvvvvvv"
+COPY_FIRST = "ss"
 COPY_REST = "ss"
 
 
@@ -145,7 +146,7 @@ def tile_testmmrsmodel_t_kernel(tc, hidden_states, gate_proj, world_size, grad_o
             else:
                 for r in range(len(stored), CHUNKS):
                     store(r, 0, TILES)
-                for r in range(len(stored)):
+                for r in reversed(range(len(stored))):
                     store(r, stored[r], TILES)
 
         def flip(t):
@@ -155,8 +156,8 @@ def tile_testmmrsmodel_t_kernel(tc, hidden_states, gate_proj, world_size, grad_o
 
         for t in range(FIRST):
             transposes(t)
-            copy_out(t, 0, "s")
-            copy_out(t, 1, "v")
+            copy_out(t, 0, COPY_FIRST[0])
+            copy_out(t, 1, COPY_FIRST[1])
             if t > 0:
                 quant_x(t - 1)
         regroup(0)

@@ -24,13 +24,13 @@ BYTES = 2 * (N_ROWS * K + K * H) + 4 * CHUNKS * N_ROWS * H
 FIRST = 2
 PIN = True
 VSHARE = [256,256,256,256]
-X_LOADS = [[0,2],[2,2],[4,2],[6,2]]
-GATE_AFTER = 1
+X_LOADS = [[0,1],[1,1],[2,2],[4,2],[6,2]]
+GATE_AFTER = 2
 EARLY = [0,3,1,1,1,1,1]
 AHEAD = 2
 RES_FIRST = "svsvsvsv"
 RES_REST = "vvvvvvvv"
-COPY_FIRST = "ss"
+COPY_FIRST = "sv"
 COPY_REST = "ss"
 
 
@@ -55,8 +55,8 @@ def tile_testmmrsmodel_t_kernel(tc, hidden_states, gate_proj, world_size, grad_o
 
         def load_g(g):
             nc.sync.dma_start(
-                out=g_raw[g][:].rearrange("p (u e) c -> p u e c", u=2),
-                in_=gate_proj[512 * g : 512 * (g + 1), :].rearrange("(u q e) c -> q u e c", u=2, e=2),
+                out=g_raw[g][:],
+                in_=gate_proj[512 * g : 512 * (g + 1), :].rearrange("(p j) c -> p j c", j=4),
             )
 
         for lo, n in X_LOADS[:GATE_AFTER]:
@@ -81,14 +81,13 @@ def tile_testmmrsmodel_t_kernel(tc, hidden_states, gate_proj, world_size, grad_o
         stored = []
 
         def transposes(t):
-            words = x_raw[t].bitcast(F32)
+            words = x_raw[t].bitcast(F32).rearrange("p (g q u) -> p g u q", g=PASSES, u=2)
             for half in range(2):
                 bank = psum_t.tile([P, 2, 2, P], F32, name="xt", tag="xt")
                 banks[(t, half)] = bank
                 for gg in range(2):
                     for u in range(2):
-                        col = 256 * (2 * half + gg) + 128 * u
-                        nc.tensor.transpose(bank[:, gg, u, :], words[:, col : col + P], ident[:])
+                        nc.tensor.transpose(bank[:, gg, u, :], words[:, 2 * half + gg, u, :], ident[:])
 
         def copy_out(t, half, engine):
             dst = x_grp[t][:].bitcast(F32).rearrange("p (g r u) -> p g r u", g=PASSES, u=2)

@@ -21,12 +21,12 @@ PASSES = K // 512
 FLOPS = 2 * N_ROWS * K * H
 BYTES = 2 * (N_ROWS * K + K * H) + 4 * CHUNKS * N_ROWS * H
 
-FIRST = 2
+FIRST = 1
 PIN = True
 VSHARE = [256,256,256,256]
-X_LOADS = [[0,1],[1,1],[2,2],[4,2],[6,2]]
-GATE_AFTER = 2
-EARLY = [0,3,1,1,1,1,1]
+X_LOADS = [[0,1],[1,1],[2,1],[3,1],[4,2],[6,2]]
+GATE_AFTER = 1
+EARLY = [1,2,2,1,1,1,0]
 AHEAD = 2
 RES_FIRST = "svsvsvsv"
 RES_REST = "vvvvvvvv"
@@ -55,8 +55,8 @@ def tile_testmmrsmodel_t_kernel(tc, hidden_states, gate_proj, world_size, grad_o
 
         def load_g(g):
             nc.sync.dma_start(
-                out=g_raw[g][:],
-                in_=gate_proj[512 * g : 512 * (g + 1), :].rearrange("(p j) c -> p j c", j=4),
+                out=g_raw[g][:].rearrange("p (u e) c -> p u e c", u=2),
+                in_=gate_proj[512 * g : 512 * (g + 1), :].rearrange("(u q e) c -> q u e c", u=2, e=2),
             )
 
         for lo, n in X_LOADS[:GATE_AFTER]:
@@ -81,13 +81,14 @@ def tile_testmmrsmodel_t_kernel(tc, hidden_states, gate_proj, world_size, grad_o
         stored = []
 
         def transposes(t):
-            words = x_raw[t].bitcast(F32).rearrange("p (g q u) -> p g u q", g=PASSES, u=2)
+            words = x_raw[t].bitcast(F32)
             for half in range(2):
                 bank = psum_t.tile([P, 2, 2, P], F32, name="xt", tag="xt")
                 banks[(t, half)] = bank
                 for gg in range(2):
                     for u in range(2):
-                        nc.tensor.transpose(bank[:, gg, u, :], words[:, 2 * half + gg, u, :], ident[:])
+                        col = 256 * (2 * half + gg) + 128 * u
+                        nc.tensor.transpose(bank[:, gg, u, :], words[:, col : col + P], ident[:])
 
         def copy_out(t, half, engine):
             dst = x_grp[t][:].bitcast(F32).rearrange("p (g r u) -> p g r u", g=PASSES, u=2)
@@ -153,32 +154,83 @@ def tile_testmmrsmodel_t_kernel(tc, hidden_states, gate_proj, world_size, grad_o
             copy_out(t, 0, COPY_REST[0])
             copy_out(t, 1, COPY_REST[1])
 
-        for t in range(FIRST):
-            transposes(t)
-            copy_out(t, 0, COPY_FIRST[0])
-            copy_out(t, 1, COPY_FIRST[1])
-            if t > 0:
-                quant_x(t - 1)
+        transposes(0)
+        copy_out(0, 0, "s")
+        copy_out(0, 1, "s")
         regroup(0)
-        quant_x(FIRST - 1)
-        for g in range(1, PASSES):
-            regroup(g)
-            quant_g(g - 1)
-            for t in range(FIRST):
-                mx_pass(t, g - 1)
-        quant_g(PASSES - 1)
-        for t in range(FIRST):
-            mx_pass(t, PASSES - 1)
-        for t in range(FIRST):
-            result(t, RES_FIRST[t])
-        for t in range(FIRST, min(FIRST + AHEAD, TILES)):
-            flip(t)
-        quant_x(FIRST)
-        for t in range(FIRST, TILES):
-            if t + AHEAD < TILES:
-                flip(t + AHEAD)
-            if t + 1 < TILES:
-                quant_x(t + 1)
-            for g in range(PASSES):
-                mx_pass(t, g)
-            result(t, RES_REST[t])
+        quant_x(0)
+        regroup(1)
+        quant_g(0)
+        mx_pass(0, 0)
+        regroup(2)
+        quant_g(1)
+        mx_pass(0, 1)
+        transposes(1)
+        regroup(3)
+        quant_g(2)
+        mx_pass(0, 2)
+        copy_out(1, 0, "s")
+        copy_out(1, 1, "s")
+        quant_g(3)
+        mx_pass(0, 3)
+        result(0, "s")
+        quant_x(1)
+        transposes(2)
+        copy_out(2, 0, "s")
+        copy_out(2, 1, "s")
+        mx_pass(1, 0)
+        mx_pass(1, 1)
+        mx_pass(1, 2)
+        mx_pass(1, 3)
+        quant_x(2)
+        result(1, "v")
+        transposes(3)
+        copy_out(3, 0, "s")
+        copy_out(3, 1, "s")
+        mx_pass(2, 0)
+        mx_pass(2, 1)
+        mx_pass(2, 2)
+        mx_pass(2, 3)
+        quant_x(3)
+        result(2, "v")
+        transposes(4)
+        copy_out(4, 0, "s")
+        copy_out(4, 1, "s")
+        transposes(5)
+        copy_out(5, 0, "s")
+        copy_out(5, 1, "s")
+        mx_pass(3, 0)
+        mx_pass(3, 1)
+        mx_pass(3, 2)
+        mx_pass(3, 3)
+        quant_x(4)
+        result(3, "v")
+        transposes(6)
+        copy_out(6, 0, "s")
+        copy_out(6, 1, "s")
+        mx_pass(4, 0)
+        mx_pass(4, 1)
+        mx_pass(4, 2)
+        mx_pass(4, 3)
+        quant_x(5)
+        result(4, "v")
+        transposes(7)
+        copy_out(7, 0, "s")
+        copy_out(7, 1, "s")
+        mx_pass(5, 0)
+        mx_pass(5, 1)
+        mx_pass(5, 2)
+        mx_pass(5, 3)
+        quant_x(6)
+        result(5, "v")
+        mx_pass(6, 0)
+        mx_pass(6, 1)
+        mx_pass(6, 2)
+        mx_pass(6, 3)
+        quant_x(7)
+        result(6, "v")
+        mx_pass(7, 0)
+        mx_pass(7, 1)
+        mx_pass(7, 2)
+        mx_pass(7, 3)
+        result(7, "v")

@@ -24,7 +24,7 @@ BYTES = 2 * (N_ROWS * K + K * H) + 4 * CHUNKS * N_ROWS * H
 FIRST = 1
 PIN = True
 VSHARE = [256,256,256,256]
-X_LOADS = [[0,1],[1,1],[2,1],[3,1],[4,2],[6,2]]
+X_LOADS = [[0,1],[1,1],[2,2],[4,2],[6,2]]
 GATE_AFTER = 1
 EARLY = [1,2,2,1,1,1,0]
 AHEAD = 2
@@ -55,8 +55,8 @@ def tile_testmmrsmodel_t_kernel(tc, hidden_states, gate_proj, world_size, grad_o
 
         def load_g(g):
             nc.sync.dma_start(
-                out=g_raw[g][:].rearrange("p (u e) c -> p u e c", u=2),
-                in_=gate_proj[512 * g : 512 * (g + 1), :].rearrange("(u q e) c -> q u e c", u=2, e=2),
+                out=g_raw[g][:],
+                in_=gate_proj[512 * g : 512 * (g + 1), :].rearrange("(p j) c -> p j c", j=4),
             )
 
         for lo, n in X_LOADS[:GATE_AFTER]:
@@ -81,14 +81,13 @@ def tile_testmmrsmodel_t_kernel(tc, hidden_states, gate_proj, world_size, grad_o
         stored = []
 
         def transposes(t):
-            words = x_raw[t].bitcast(F32)
+            words = x_raw[t].bitcast(F32).rearrange("p (g q u) -> p g u q", g=PASSES, u=2)
             for half in range(2):
                 bank = psum_t.tile([P, 2, 2, P], F32, name="xt", tag="xt")
                 banks[(t, half)] = bank
                 for gg in range(2):
                     for u in range(2):
-                        col = 256 * (2 * half + gg) + 128 * u
-                        nc.tensor.transpose(bank[:, gg, u, :], words[:, col : col + P], ident[:])
+                        nc.tensor.transpose(bank[:, gg, u, :], words[:, 2 * half + gg, u, :], ident[:])
 
         def copy_out(t, half, engine):
             dst = x_grp[t][:].bitcast(F32).rearrange("p (g r u) -> p g r u", g=PASSES, u=2)

@@ -24,7 +24,7 @@ BYTES = 2 * (N_ROWS * K + K * H) + 4 * CHUNKS * N_ROWS * H
 FIRST = 1
 PIN = True
 VSHARE = [256,256,256,256]
-X_LOADS = [[0,1],[1,1],[2,2],[4,2],[6,2]]
+X_LOADS = [[0,1],[1,1],[2,1],[3,1],[4,2],[6,2]]
 GATE_AFTER = 1
 EARLY = [1,2,2,1,1,1,0]
 AHEAD = 2
@@ -55,8 +55,8 @@ def tile_testmmrsmodel_t_kernel(tc, hidden_states, gate_proj, world_size, grad_o
 
         def load_g(g):
             nc.sync.dma_start(
-                out=g_raw[g][:],
-                in_=gate_proj[512 * g : 512 * (g + 1), :].rearrange("(p j) c -> p j c", j=4),
+                out=g_raw[g][:].rearrange("p (u e) c -> p u e c", u=2),
+                in_=gate_proj[512 * g : 512 * (g + 1), :].rearrange("(u q e) c -> q u e c", u=2, e=2),
             )
 
         for lo, n in X_LOADS[:GATE_AFTER]:
@@ -81,13 +81,14 @@ def tile_testmmrsmodel_t_kernel(tc, hidden_states, gate_proj, world_size, grad_o
         stored = []
 
         def transposes(t):
-            words = x_raw[t].bitcast(F32).rearrange("p (g q u) -> p g u q", g=PASSES, u=2)
+            words = x_raw[t].bitcast(F32)
             for half in range(2):
                 bank = psum_t.tile([P, 2, 2, P], F32, name="xt", tag="xt")
                 banks[(t, half)] = bank
                 for gg in range(2):
                     for u in range(2):
-                        nc.tensor.transpose(bank[:, gg, u, :], words[:, 2 * half + gg, u, :], ident[:])
+                        col = 256 * (2 * half + gg) + 128 * u
+                        nc.tensor.transpose(bank[:, gg, u, :], words[:, col : col + P], ident[:])
 
         def copy_out(t, half, engine):
             dst = x_grp[t][:].bitcast(F32).rearrange("p (g r u) -> p g r u", g=PASSES, u=2)
@@ -128,8 +129,8 @@ def tile_testmmrsmodel_t_kernel(tc, hidden_states, gate_proj, world_size, grad_o
                 stop=(g == PASSES - 1),
             )
 
-        def store(r, lo, hi):
-            nc.sync.dma_start(
+        def store(r, lo, hi, queue=None):
+            (queue or nc.sync).dma_start(
                 out=out[r].rearrange("(p t) h -> p t h", t=TILES)[:, lo:hi, :], in_=res[:, lo:hi, :]
             )
 
@@ -143,10 +144,10 @@ def tile_testmmrsmodel_t_kernel(tc, hidden_states, gate_proj, world_size, grad_o
                     store(len(stored), 0, t + 1)
                     stored.append(t + 1)
             else:
-                for r in range(len(stored), CHUNKS):
-                    store(r, 0, TILES)
-                for r in reversed(range(len(stored))):
-                    store(r, stored[r], TILES)
+                late = [(r, 0) for r in range(len(stored), CHUNKS)]
+                late.extend([(r, stored[r]) for r in reversed(range(len(stored)))])
+                for i, (r, lo) in enumerate(late):
+                    store(r, lo, TILES, nc.scalar if i % 2 else nc.sync)
 
         def flip(t):
             transposes(t)

@@ -21,17 +21,11 @@ PASSES = K // 512
 FLOPS = 2 * N_ROWS * K * H
 BYTES = 2 * (N_ROWS * K + K * H) + 4 * CHUNKS * N_ROWS * H
 
-FIRST = 1
 PIN = True
 VSHARE = [256,256,256,256]
 X_LOADS = [[0,1],[1,1],[2,1],[3,1],[4,2],[6,2]]
 GATE_AFTER = 1
-EARLY = [1,2,2,1,1,1,0]
-AHEAD = 2
-RES_FIRST = "svsvsvsv"
-RES_REST = "vvvvvvvv"
-COPY_FIRST = "sv"
-COPY_REST = "ss"
+STEPS = {0: [0, 1, 2, 3], 1: [4, 5, 6, 7], 3: [0, 1, 2, 3], 7: [0, 1, 2, 3, 4, 5, 6, 7]}
 
 
 def tile_testmmrsmodel_t_kernel(tc, hidden_states, gate_proj, world_size, grad_out, out):
@@ -78,7 +72,7 @@ def tile_testmmrsmodel_t_kernel(tc, hidden_states, gate_proj, world_size, grad_o
         res = keep.tile([P, TILES, H], F32, name="res")
         banks = {}
         accs = {}
-        stored = []
+        stored = [0] * CHUNKS
 
         def transposes(t):
             words = x_raw[t].bitcast(F32)
@@ -139,20 +133,9 @@ def tile_testmmrsmodel_t_kernel(tc, hidden_states, gate_proj, world_size, grad_o
                 nc.vector.tensor_copy(out=res[:, t, :], in_=accs[t][:])
             else:
                 nc.scalar.copy(out=res[:, t, :], in_=accs[t][:])
-            if t < TILES - 1:
-                for i in range(EARLY[t]):
-                    store(len(stored), 0, t + 1)
-                    stored.append(t + 1)
-            else:
-                late = [(r, 0) for r in range(len(stored), CHUNKS)]
-                late.extend([(r, stored[r]) for r in reversed(range(len(stored)))])
-                for i, (r, lo) in enumerate(late):
-                    store(r, lo, TILES, nc.scalar if i % 2 else nc.sync)
-
-        def flip(t):
-            transposes(t)
-            copy_out(t, 0, COPY_REST[0])
-            copy_out(t, 1, COPY_REST[1])
+            for i, r in enumerate(STEPS.get(t, [])):
+                store(r, stored[r], t + 1, nc.scalar if t == TILES - 1 and i % 2 else nc.sync)
+                stored[r] = t + 1
 
         transposes(0)
         copy_out(0, 0, "s")

@@ -39,10 +39,10 @@ def tile_testmmrsmodel_t_kernel(tc, hidden_states, gate_proj, world_size, grad_o
 
         x_rows = grad_out.rearrange("(p t) k -> p t k", t=TILES)
         x_raw = {}
-        g_raw = [keep.tile([P, 4, H], BF16, name="g_raw%d" % g) for g in range(PASSES)]
+        g_raw = [keep.tile([P, 4, H], BF16, name="g_raw%d" % g, align_bytes=512) for g in range(PASSES)]
 
         def load_x(lo, n):
-            raw = keep.tile([P, n, K], BF16, name="x_raw%d" % lo)
+            raw = keep.tile([P, n, K], BF16, name="x_raw%d" % lo, align_bytes=512)
             nc.sync.dma_start(out=raw[:], in_=x_rows[:, lo : lo + n, :])
             for j in range(n):
                 x_raw[lo + j] = raw[:, j, :]
@@ -69,7 +69,7 @@ def tile_testmmrsmodel_t_kernel(tc, hidden_states, gate_proj, world_size, grad_o
         g_grp = [keep.tile([P, H, 4], BF16, name="g_grp%d" % g, align_bytes=64) for g in range(PASSES)]
         g_code = [keep.tile([P, H], U32, name="g_code%d" % g, align_bytes=64) for g in range(PASSES)]
         g_scale = [keep.tile([P, H], U8, name="g_scale%d" % g, align_bytes=64) for g in range(PASSES)]
-        res = keep.tile([P, TILES, H], F32, name="res")
+        res = keep.tile([P, TILES, H], F32, name="res", align_bytes=512)
         banks = {}
         accs = {}
         stored = [0] * CHUNKS

@@ -22,10 +22,8 @@ FLOPS = 2 * N_ROWS * K * H
 BYTES = 2 * (N_ROWS * K + K * H) + 4 * CHUNKS * N_ROWS * H
 
 PIN = True
-VSHARE = [256,256,256,256]
-X_LOADS = [[0,1],[1,1],[2,1],[3,1],[4,2],[6,2]]
-GATE_AFTER = 1
-STEPS = {0: [0, 1, 2, 3], 1: [4, 5, 6, 7], 3: [0, 1, 2, 3], 7: [0, 1, 2, 3, 4, 5, 6, 7]}
+VSHARE = [320, 256, 256, 256]
+STEPS = {1: [0, 1, 2], 2: [3], 3: [4], 4: [5], 5: [6], 7: [7, 6, 5, 4, 3, 2, 1, 0]}
 
 
 def tile_testmmrsmodel_t_kernel(tc, hidden_states, gate_proj, world_size, grad_out, out):
@@ -49,16 +47,19 @@ def tile_testmmrsmodel_t_kernel(tc, hidden_states, gate_proj, world_size, grad_o
 
         def load_g(g):
             nc.sync.dma_start(
-                out=g_raw[g][:].rearrange("p (u e) c -> p u e c", u=2),
-                in_=gate_proj[512 * g : 512 * (g + 1), :].rearrange("(u q e) c -> q u e c", u=2, e=2),
+                out=g_raw[g][:],
+                in_=gate_proj[512 * g : 512 * (g + 1), :].rearrange("(q e) c -> q e c", e=4),
             )
 
-        for lo, n in X_LOADS[:GATE_AFTER]:
-            load_x(lo, n)
-        for g in range(PASSES):
-            load_g(g)
-        for lo, n in X_LOADS[GATE_AFTER:]:
-            load_x(lo, n)
+        load_x(0, 1)
+        load_x(1, 1)
+        load_g(0)
+        load_g(1)
+        load_g(2)
+        load_x(2, 1)
+        load_g(3)
+        load_x(3, 1)
+        load_x(4, 4)
 
         ident = keep.tile([P, P], F32, name="ident")
         make_identity(nc, ident[:])
@@ -81,8 +82,8 @@ def tile_testmmrsmodel_t_kernel(tc, hidden_states, gate_proj, world_size, grad_o
                 banks[(t, half)] = bank
                 for gg in range(2):
                     for u in range(2):
-                        col = 256 * (2 * half + gg) + 128 * u
-                        nc.tensor.transpose(bank[:, gg, u, :], words[:, col : col + P], ident[:])
+                        col = 256 * (2 * half + gg)
+                        nc.tensor.transpose(bank[:, gg, u, :], words[:, col + u : col + 256 : 2], ident[:])
 
         def copy_out(t, half, engine):
             dst = x_grp[t][:].bitcast(F32).rearrange("p (g r u) -> p g r u", g=PASSES, u=2)
@@ -138,82 +139,45 @@ def tile_testmmrsmodel_t_kernel(tc, hidden_states, gate_proj, world_size, grad_o
                 stored[r] = t + 1
 
         transposes(0)
-        copy_out(0, 0, "s")
+        copy_out(0, 0, "v")
         copy_out(0, 1, "s")
-        regroup(0)
         quant_x(0)
+        transposes(1)
+        copy_out(1, 0, "s")
+        copy_out(1, 1, "s")
+        regroup(0)
+        quant_x(1)
         regroup(1)
         quant_g(0)
+        transposes(2)
         mx_pass(0, 0)
+        mx_pass(1, 0)
         regroup(2)
         quant_g(1)
         mx_pass(0, 1)
-        transposes(1)
+        mx_pass(1, 1)
         regroup(3)
         quant_g(2)
         mx_pass(0, 2)
-        copy_out(1, 0, "s")
-        copy_out(1, 1, "s")
+        mx_pass(1, 2)
         quant_g(3)
         mx_pass(0, 3)
-        result(0, "s")
-        quant_x(1)
-        transposes(2)
+        mx_pass(1, 3)
         copy_out(2, 0, "s")
         copy_out(2, 1, "s")
-        mx_pass(1, 0)
-        mx_pass(1, 1)
-        mx_pass(1, 2)
-        mx_pass(1, 3)
+        result(0, "v")
         quant_x(2)
-        result(1, "v")
+        result(1, "s")
         transposes(3)
         copy_out(3, 0, "s")
         copy_out(3, 1, "s")
-        mx_pass(2, 0)
-        mx_pass(2, 1)
-        mx_pass(2, 2)
-        mx_pass(2, 3)
-        quant_x(3)
-        result(2, "v")
-        transposes(4)
-        copy_out(4, 0, "s")
-        copy_out(4, 1, "s")
-        transposes(5)
-        copy_out(5, 0, "s")
-        copy_out(5, 1, "s")
-        mx_pass(3, 0)
-        mx_pass(3, 1)
-        mx_pass(3, 2)
-        mx_pass(3, 3)
-        quant_x(4)
-        result(3, "v")
-        transposes(6)
-        copy_out(6, 0, "s")
-        copy_out(6, 1, "s")
-        mx_pass(4, 0)
-        mx_pass(4, 1)
-        mx_pass(4, 2)
-        mx_pass(4, 3)
-        quant_x(5)
-        result(4, "v")
-        transposes(7)
-        copy_out(7, 0, "s")
-        copy_out(7, 1, "s")
-        mx_pass(5, 0)
-        mx_pass(5, 1)
-        mx_pass(5, 2)
-        mx_pass(5, 3)
-        quant_x(6)
-        result(5, "v")
-        mx_pass(6, 0)
-        mx_pass(6, 1)
-        mx_pass(6, 2)
-        mx_pass(6, 3)
-        quant_x(7)
-        result(6, "v")
-        mx_pass(7, 0)
-        mx_pass(7, 1)
-        mx_pass(7, 2)
-        mx_pass(7, 3)
-        result(7, "v")
+        for t in range(2, TILES):
+            for g in range(PASSES):
+                mx_pass(t, g)
+            if t + 2 < TILES:
+                transposes(t + 2)
+                copy_out(t + 2, 0, "s")
+                copy_out(t + 2, 1, "s")
+            if t + 1 < TILES:
+                quant_x(t + 1)
+            result(t, "v")

@@ -23,7 +23,7 @@ BYTES = 2 * (N_ROWS * K + K * H) + 4 * CHUNKS * N_ROWS * H
 
 PIN = True
 VSHARE = [320, 256, 256, 256]
-STEPS = {1: [0, 1, 2], 2: [3], 3: [4], 4: [5], 5: [6], 7: [7, 6, 5, 4, 3, 2, 1, 0]}
+STEPS = {1: [0, 1, 2, 3], 2: [4], 3: [5], 4: [6], 5: [7], 7: [7, 6, 5, 4, 3, 2, 1, 0]}
 
 
 def tile_testmmrsmodel_t_kernel(tc, hidden_states, gate_proj, world_size, grad_out, out):
@@ -37,10 +37,10 @@ def tile_testmmrsmodel_t_kernel(tc, hidden_states, gate_proj, world_size, grad_o
 
         x_rows = grad_out.rearrange("(p t) k -> p t k", t=TILES)
         x_raw = {}
-        g_raw = [keep.tile([P, 4, H], BF16, name="g_raw%d" % g, align_bytes=512) for g in range(PASSES)]
+        g_raw = [keep.tile([P, 4, H], BF16, name="g_raw%d" % g, align_bytes=4096) for g in range(PASSES)]
 
         def load_x(lo, n):
-            raw = keep.tile([P, n, K], BF16, name="x_raw%d" % lo, align_bytes=512)
+            raw = keep.tile([P, n, K], BF16, name="x_raw%d" % lo, align_bytes=4096)
             nc.sync.dma_start(out=raw[:], in_=x_rows[:, lo : lo + n, :])
             for j in range(n):
                 x_raw[lo + j] = raw[:, j, :]
@@ -70,7 +70,7 @@ def tile_testmmrsmodel_t_kernel(tc, hidden_states, gate_proj, world_size, grad_o
         g_grp = [keep.tile([P, H, 4], BF16, name="g_grp%d" % g, align_bytes=64) for g in range(PASSES)]
         g_code = [keep.tile([P, H], U32, name="g_code%d" % g, align_bytes=64) for g in range(PASSES)]
         g_scale = [keep.tile([P, H], U8, name="g_scale%d" % g, align_bytes=64) for g in range(PASSES)]
-        res = keep.tile([P, TILES, H], F32, name="res", align_bytes=512)
+        res = keep.tile([P, TILES, H], F32, name="res", align_bytes=4096)
         banks = {}
         accs = {}
         stored = [0] * CHUNKS

from contextlib import ExitStack

import concourse.mybir as mybir
from concourse.masks import make_identity

BF16 = mybir.dt.bfloat16
F32 = mybir.dt.float32
U32 = mybir.dt.uint32
U8 = mybir.dt.uint8
E4M3X4 = mybir.dt.float8_e4m3fn_x4
E5M2X4 = mybir.dt.float8_e5m2_x4

P = 128
N_ROWS = 1024
K = 2048
H = 512
CHUNKS = 8
TILES = N_ROWS // P
PASSES = K // 512

FLOPS = 2 * N_ROWS * K * H
BYTES = 2 * (N_ROWS * K + K * H) + 4 * CHUNKS * N_ROWS * H

PIN = True
VSHARE = [320, 256, 256, 256]
STEPS = {1: [0, 1, 2, 3], 2: [4], 3: [5], 4: [6], 5: [7], 7: [7, 6, 5, 4, 3, 2, 1, 0]}


def tile_testmmrsmodel_t_kernel(tc, hidden_states, gate_proj, world_size, grad_out, out):
    nc = tc.nc
    with ExitStack() as ctx:
        keep = ctx.enter_context(tc.tile_pool(name="keep", bufs=1))
        psum_t = ctx.enter_context(tc.psum_pool(name="psum_t", bufs=4))
        psum_a = ctx.enter_context(tc.psum_pool(name="psum_a", bufs=4))
        if PIN:
            ctx.enter_context(tc.manual_schedule())

        x_rows = grad_out.rearrange("(p t) k -> p t k", t=TILES)
        x_raw = {}
        g_raw = [keep.tile([P, 4, H], BF16, name="g_raw%d" % g, align_bytes=4096) for g in range(PASSES)]

        def load_x(lo, n):
            raw = keep.tile([P, n, K], BF16, name="x_raw%d" % lo, align_bytes=4096)
            nc.sync.dma_start(out=raw[:], in_=x_rows[:, lo : lo + n, :])
            for j in range(n):
                x_raw[lo + j] = raw[:, j, :]

        def load_g(g):
            nc.sync.dma_start(
                out=g_raw[g][:],
                in_=gate_proj[512 * g : 512 * (g + 1), :].rearrange("(q e) c -> q e c", e=4),
            )

        load_x(0, 1)
        load_x(1, 1)
        load_g(0)
        load_g(1)
        load_g(2)
        load_x(2, 1)
        load_g(3)
        load_x(3, 1)
        load_x(4, 4)

        ident = keep.tile([P, P], F32, name="ident")
        make_identity(nc, ident[:])

        x_grp = [keep.tile([P, K], BF16, name="x_grp%d" % t, align_bytes=64) for t in range(TILES)]
        x_code = [keep.tile([P, K // 4], U32, name="x_code%d" % t, align_bytes=64) for t in range(TILES)]
        x_scale = [keep.tile([P, K // 4], U8, name="x_scale%d" % t, align_bytes=64) for t in range(TILES)]
        g_grp = [keep.tile([P, H, 4], BF16, name="g_grp%d" % g, align_bytes=64) for g in range(PASSES)]
        g_code = [keep.tile([P, H], U32, name="g_code%d" % g, align_bytes=64) for g in range(PASSES)]
        g_scale = [keep.tile([P, H], U8, name="g_scale%d" % g, align_bytes=64) for g in range(PASSES)]
        res = keep.tile([P, TILES, H], F32, name="res", align_bytes=4096)
        banks = {}
        accs = {}
        stored = [0] * CHUNKS

        def transposes(t):
            words = x_raw[t].bitcast(F32)
            for half in range(2):
                bank = psum_t.tile([P, 2, 2, P], F32, name="xt", tag="xt")
                banks[(t, half)] = bank
                for gg in range(2):
                    for u in range(2):
                        col = 256 * (2 * half + gg)
                        nc.tensor.transpose(bank[:, gg, u, :], words[:, col + u : col + 256 : 2], ident[:])

        def copy_out(t, half, engine):
            dst = x_grp[t][:].bitcast(F32).rearrange("p (g r u) -> p g r u", g=PASSES, u=2)
            src = banks[(t, half)][:].rearrange("p g u r -> p g r u")
            if engine == "v":
                nc.vector.tensor_copy(out=dst[:, 2 * half : 2 * half + 2], in_=src)
            else:
                nc.scalar.copy(out=dst[:, 2 * half : 2 * half + 2], in_=src)

        def quant_x(t):
            nc.vector.quantize_mx(out=x_code[t][:].bitcast(E5M2X4), scales=x_scale[t][:], in_=x_grp[t][:])

        def regroup(g):
            dst = g_grp[g][:].rearrange("p (c i) t -> p c t i", i=4)
            src = g_raw[g][:].rearrange("p t (c i) -> p c t i", i=4)
            cut = VSHARE[g] // 4
            nc.vector.tensor_copy(out=dst[:, 0:cut], in_=src[:, 0:cut])
            if cut < H // 4:
                nc.scalar.copy(out=dst[:, cut:], in_=src[:, cut:])

        def quant_g(g):
            nc.vector.quantize_mx(
                out=g_code[g][:].bitcast(E4M3X4),
                scales=g_scale[g][:],
                in_=g_grp[g][:].rearrange("p c t -> p (c t)"),
            )

        def mx_pass(t, g):
            if g == 0:
                accs[t] = psum_a.tile([P, H], F32, name="acc", tag="acc")
            nc.tensor.matmul_mx(
                out=accs[t][:],
                lhsT=x_code[t][:, P * g : P * (g + 1)].bitcast(E5M2X4),
                lhsT_scale=x_scale[t][:, P * g : P * (g + 1)],
                rhs=g_code[g][:].bitcast(E4M3X4),
                rhs_scale=g_scale[g][:],
                start=(g == 0),
                stop=(g == PASSES - 1),
            )

        def store(r, lo, hi, queue=None):
            (queue or nc.sync).dma_start(
                out=out[r].rearrange("(p t) h -> p t h", t=TILES)[:, lo:hi, :], in_=res[:, lo:hi, :]
            )

        def result(t, engine):
            if engine == "v":
                nc.vector.tensor_copy(out=res[:, t, :], in_=accs[t][:])
            else:
                nc.scalar.copy(out=res[:, t, :], in_=accs[t][:])
            for i, r in enumerate(STEPS.get(t, [])):
                store(r, stored[r], t + 1, nc.scalar if t == TILES - 1 and i % 2 else nc.sync)
                stored[r] = t + 1

        transposes(0)
        copy_out(0, 0, "v")
        copy_out(0, 1, "s")
        quant_x(0)
        transposes(1)
        copy_out(1, 0, "s")
        copy_out(1, 1, "s")
        regroup(0)
        quant_x(1)
        regroup(1)
        quant_g(0)
        transposes(2)
        mx_pass(0, 0)
        mx_pass(1, 0)
        regroup(2)
        quant_g(1)
        mx_pass(0, 1)
        mx_pass(1, 1)
        regroup(3)
        quant_g(2)
        mx_pass(0, 2)
        mx_pass(1, 2)
        quant_g(3)
        mx_pass(0, 3)
        mx_pass(1, 3)
        copy_out(2, 0, "s")
        copy_out(2, 1, "s")
        result(0, "v")
        quant_x(2)
        result(1, "s")
        transposes(3)
        copy_out(3, 0, "s")
        copy_out(3, 1, "s")
        for t in range(2, TILES):
            for g in range(PASSES):
                mx_pass(t, g)
            if t + 2 < TILES:
                transposes(t + 2)
                copy_out(t + 2, 0, "s")
                copy_out(t + 2, 1, "s")
            if t + 1 < TILES:
                quant_x(t + 1)
            result(t, "v")
